import numpy as np
import ml_dtypes


def mxq(x, axis, fmt="e4m3"):
    dtype, down = {"e4m3": (ml_dtypes.float8_e4m3fn, 7), "e5m2": (ml_dtypes.float8_e5m2, 14)}[fmt]
    v = np.moveaxis(np.asarray(x, np.float32).astype(ml_dtypes.bfloat16).astype(np.float64), axis, -1)
    blocks = v.reshape(v.shape[:-1] + (-1, 32))
    amax = np.abs(blocks).max(-1, keepdims=True)
    byte = np.maximum(np.where(amax > 0, np.frexp(amax)[1] - 1 + 127, 0) - down, 1)
    scale = np.exp2(byte - 127.0)
    codes = (blocks / scale).astype(np.float32).astype(dtype).astype(np.float64)
    return np.moveaxis((codes * scale).reshape(v.shape), -1, axis)


WIDE = False


def mx_kscale(k):
    if not WIDE:
        return np.ones(k)
    levels = np.array([10, -10, 5, -5, 0])
    a = np.random.permutation(np.resize(levels, k // 512 * 4)).reshape(k // 512, 4)
    idx = np.arange(k)
    return np.exp2(a[idx // 512, idx % 128 // 32])


BF16 = ml_dtypes.bfloat16


def bf(x):
    return np.asarray(x, np.float32).astype(BF16)


def f64(x):
    return np.asarray(x).astype(np.float64)


E2M1 = np.array([0.0, 0.5, 1.0, 1.5, 2.0, 3.0, 4.0, 6.0, -0.0, -0.5, -1.0, -1.5, -2.0, -3.0, -4.0, -6.0])


def pack_weight(w, fmt):
    k, n = w.shape
    w = f64(bf(w)).reshape(k // 32, 32, n)
    amax = np.abs(w).max(1)
    if fmt == "e4m3":
        byte = np.frexp(amax)[1] - 1 + 127 - 7
    else:
        mant, ex = np.frexp(amax / 6.0)
        byte = np.where(mant > 0.5, ex, ex - 1) + 127
    byte = np.clip(np.where(amax > 0, byte, 1), 1, 254)
    scaled = (w * np.exp2(127.0 - byte)[:, None, :]).reshape(k, n).astype(np.float32)
    by_word = np.ascontiguousarray(scaled.reshape(k // 512, 128, 4, n).transpose(0, 1, 3, 2))
    if fmt == "e4m3":
        words = by_word.astype(ml_dtypes.float8_e4m3fn).view(np.uint8)
    else:
        c = by_word.astype(ml_dtypes.float4_e2m1fn).view(np.uint8) & 0xF
        words = c[..., 0::2] | (c[..., 1::2] << 4)
    return np.ascontiguousarray(words), np.ascontiguousarray(byte.astype(np.uint8).reshape(k // 512, 16, n))


def unpack_weight(words, scales, fmt):
    g, p, n, _ = words.shape
    if fmt == "e4m3":
        vals = np.ascontiguousarray(words).view(ml_dtypes.float8_e4m3fn).astype(np.float64)
    else:
        nib = np.empty((g, p, n, 4), np.uint8)
        nib[..., 0::2] = words & 0xF
        nib[..., 1::2] = words >> 4
        vals = E2M1[nib]
    vals = vals * np.repeat(np.exp2(scales.astype(np.float64) - 127.0), 8, axis=1)[..., None]
    return vals.transpose(0, 1, 3, 2).reshape(g * 512, n)

def pack4(w):
    words, scales = pack_weight(w, "e2m1")
    return words.reshape(words.shape[0], 128, -1), scales


def unpack4(words, scales):
    return unpack_weight(words.reshape(words.shape[0], 128, -1, 2), scales, "e2m1")


B, N, AB, MAXN, BB, H = 2, 32, 352, 255, 32, 1024
TAIL = AB - (MAXN + 1)
AF = AB + TAIL
FB = AF + BB + BB


def setup_inputs():
    s = mx_kscale(FB)
    sa, sb = s[:AB], s[AF:AF + BB]
    se = np.concatenate([sa, sa[MAXN + 1:], sb, sb])
    f_atoms = bf(np.random.standard_normal((B, N, AB)) * sa)
    f_bonds = bf(np.random.standard_normal((B, N, N, BB)) * sb)
    adj = bf(np.random.uniform(size=(B, N, N)) * 4.0 / N)
    w = np.random.standard_normal((H, FB)) * 0.1 * N / np.sqrt(FB) / se
    words, scales = pack4(np.ascontiguousarray(w.T))
    return {"f_atoms": f_atoms,
            "f_bonds": f_bonds,
            "adj": adj,
            "W_i_w_words": words,
            "W_i_w_scales": scales}


def reference(f_atoms, f_bonds, adj, W_i_w_words, W_i_w_scales):
    f_atoms, f_bonds, adj = f64(f_atoms), f64(f_bonds), f64(adj)
    fa = np.concatenate([f_atoms, f_atoms[:, :, MAXN + 1:]], axis=-1)
    fa_exp = np.broadcast_to(fa[:, :, None, :], (B, N, N, AF))
    fb = np.concatenate([fa_exp, f_bonds, f_bonds], axis=-1)
    return mxq(adj[..., None] * fb, 3, "e4m3") @ unpack4(W_i_w_words, W_i_w_scales)

@@ -1,0 +1,160 @@
+from contextlib import ExitStack
+
+import concourse.mybir as mybir
+from concourse.masks import make_identity
+
+BF16 = mybir.dt.bfloat16
+F32 = mybir.dt.float32
+I32 = mybir.dt.int32
+U32 = mybir.dt.uint32
+U8 = mybir.dt.uint8
+FP8X4 = mybir.dt.float8_e4m3fn_x4
+FP4X4 = mybir.dt.float4_e2m1fn_x4
+MULT = mybir.AluOpType.mult
+
+P = 128
+PACK = 4
+PAIRS = 2 * 32 * 32
+TILES = PAIRS // P
+ATOM = 352
+TAIL = 96
+BOND = 32
+ATOM_K = (ATOM + TAIL) // PACK
+BOND_K = BOND // PACK
+HIDDEN = 1024
+BANK = 512
+LEAD = 2
+
+FLOPS = 2 * PAIRS * 512 * HIDDEN
+
+
+def tile_mpnencoder_pa_kernel(tc, f_atoms, f_bonds, adj, w_words, w_scales, out):
+    nc = tc.nc
+    groups = [(j, 1) for j in range(LEAD)] + [(j, 2) for j in range(LEAD, TILES, 2)]
+
+    with ExitStack() as ctx:
+        keep = ctx.enter_context(tc.tile_pool(name="keep", bufs=1))
+        flipped_pool = ctx.enter_context(tc.psum_pool(name="flipped", bufs=2))
+        acc_pool = ctx.enter_context(tc.psum_pool(name="acc", bufs=6))
+        ctx.enter_context(tc.manual_schedule())
+
+        adj_sb = keep.tile([P, TILES], BF16, name="adj_sb")
+        atoms = keep.tile([P, ATOM], BF16, name="atoms")
+        bonds = keep.tile([P, TILES, BOND], BF16, name="bonds")
+        weight = keep.tile([P, 2 * HIDDEN], U8, name="weight", align_bytes=64)
+        weight_scales = keep.tile([P, HIDDEN], U8, name="weight_scales", align_bytes=64)
+
+        nc.vector.memset(weight_scales[:].bitcast(I32), 0)
+
+        nc.scalar.dma_start(out=adj_sb[:], in_=adj.rearrange("b m (h j) -> (b m h) j", j=TILES))
+        nc.scalar.dma_start(
+            out=atoms[:],
+            in_=f_atoms.rearrange("b m f -> (b m) f").unsqueeze(1).to_broadcast([P // 2, 2, ATOM]),
+        )
+        nc.scalar.dma_start(out=bonds[:], in_=f_bonds.rearrange("b m (h j) f -> (b m h) j f", j=TILES))
+        nc.sync.dma_start(out=weight[:].bitcast(I32), in_=w_words[0].bitcast(I32))
+        for q in range(4):
+            nc.sync.dma_start(
+                out=weight_scales[32 * q : 32 * q + 4, :].bitcast(I32),
+                in_=w_scales[0, 4 * q : 4 * q + 4, :].bitcast(I32),
+            )
+
+        identity = keep.tile([P, P], BF16, name="identity")
+        make_identity(nc, identity[:])
+
+        adj_f32 = keep.tile([P, TILES], F32, name="adj_f32")
+        nc.vector.tensor_copy(out=adj_f32[:], in_=adj_sb[:])
+        sorted_atoms = keep.tile([P, PACK, ATOM_K], BF16, name="sorted_atoms")
+        nc.scalar.copy(
+            out=sorted_atoms[:, :, 0 : ATOM // PACK],
+            in_=atoms[:].rearrange("p (k t) -> p t k", t=PACK),
+        )
+        nc.scalar.copy(
+            out=sorted_atoms[:, :, ATOM // PACK : ATOM_K],
+            in_=atoms[:, ATOM - TAIL : ATOM].rearrange("p (k t) -> p t k", t=PACK),
+        )
+
+        gated = keep.tile([P, TILES, PACK, P], BF16, name="gated")
+        grouped = keep.tile([P, TILES, P, PACK], BF16, name="grouped", align_bytes=64)
+        codes = keep.tile([P, TILES, P], U32, name="codes", align_bytes=64)
+        scales = keep.tile([P, TILES, P], U8, name="scales", align_bytes=64)
+        result = keep.tile([P, TILES, HIDDEN], F32, name="result")
+        out_rows = out.rearrange("b m (h j) c -> (b m h) j c", j=TILES)
+        flipped = {}
+
+        def gate(first, count):
+            for j in range(first, first + count):
+                nc.vector.tensor_scalar(
+                    out=gated[:, j, :, 0:ATOM_K],
+                    in0=sorted_atoms[:],
+                    scalar1=adj_f32[:, j : j + 1],
+                    scalar2=None,
+                    op0=MULT,
+                )
+                nc.vector.tensor_scalar(
+                    out=gated[:, j, :, ATOM_K:P].rearrange("p t (d k) -> p t d k", d=2),
+                    in0=bonds[:, j, :]
+                    .rearrange("p (k t) -> p t k", t=PACK)
+                    .unsqueeze(2)
+                    .to_broadcast([P, PACK, 2, BOND_K]),
+                    scalar1=adj_f32[:, j : j + 1],
+                    scalar2=None,
+                    op0=MULT,
+                )
+
+        def flip(first, count):
+            bank = flipped_pool.tile([P, count, PACK, P], BF16, name="bank", tag="bank")
+            flipped[first] = bank
+            for i in range(count):
+                for t in range(PACK):
+                    nc.tensor.transpose(bank[:, i, t, :], gated[:, first + i, t, :], identity[:])
+
+        def regroup(first, count):
+            nc.scalar.copy(
+                out=grouped[:, first : first + count, :, :],
+                in_=flipped[first][:].rearrange("k i t p -> k i p t"),
+            )
+
+        def quantise(first, count):
+            nc.vector.quantize_mx(
+                out=codes[:, first : first + count, :].rearrange("k i p -> k (i p)").bitcast(FP8X4),
+                scales=scales[:, first : first + count, :].rearrange("k i p -> k (i p)"),
+                in_=grouped[:, first : first + count, :, :].rearrange("k i p t -> k (i p t)"),
+            )
+
+        def project(first, count):
+            for j in range(first, first + count):
+                for half in range(HIDDEN // BANK):
+                    acc = acc_pool.tile([P, BANK], F32, name="acc", tag="acc")
+                    nc.tensor.matmul_mx(
+                        out=acc[:],
+                        lhsT=codes[:, j, :].bitcast(FP8X4),
+                        lhsT_scale=scales[:, j, :],
+                        rhs=weight[:, 2 * BANK * half : 2 * BANK * (half + 1)].bitcast(FP4X4),
+                        rhs_scale=weight_scales[:, BANK * half : BANK * (half + 1)],
+                        start=True,
+                        stop=True,
+                    )
+                    columns = result[:, j, BANK * half : BANK * (half + 1)]
+                    if half == 0:
+                        nc.vector.tensor_copy(out=columns, in_=acc[:])
+                    else:
+                        nc.scalar.copy(out=columns, in_=acc[:])
+                nc.sync.dma_start(out=out_rows[:, j, :], in_=result[:, j, :])
+
+        n = len(groups)
+        for i in range(3):
+            gate(*groups[i])
+        for i in range(2):
+            flip(*groups[i])
+            regroup(*groups[i])
+        quantise(*groups[0])
+        for i in range(n):
+            if i + 3 < n:
+                gate(*groups[i + 3])
+            if i + 2 < n:
+                flip(*groups[i + 2])
+                regroup(*groups[i + 2])
+            if i + 1 < n:
+                quantise(*groups[i + 1])
+            project(*groups[i])

@@ -23,14 +23,12 @@ ATOM_K = (ATOM + TAIL) // PACK
 BOND_K = BOND // PACK
 HIDDEN = 1024
 BANK = 512
-LEAD = 2
 
 FLOPS = 2 * PAIRS * 512 * HIDDEN
 
 
 def tile_mpnencoder_pa_kernel(tc, f_atoms, f_bonds, adj, w_words, w_scales, out):
     nc = tc.nc
-    groups = [(j, 1) for j in range(LEAD)] + [(j, 2) for j in range(LEAD, TILES, 2)]
 
     with ExitStack() as ctx:
         keep = ctx.enter_context(tc.tile_pool(name="keep", bufs=1))
@@ -46,11 +44,11 @@ def tile_mpnencoder_pa_kernel(tc, f_atoms, f_bonds, adj, w_words, w_scales, out)
 
         nc.vector.memset(weight_scales[:].bitcast(I32), 0)
 
-        nc.scalar.dma_start(out=adj_sb[:], in_=adj.rearrange("b m (h j) -> (b m h) j", j=TILES))
-        nc.scalar.dma_start(
+        nc.sync.dma_start(
             out=atoms[:],
             in_=f_atoms.rearrange("b m f -> (b m) f").unsqueeze(1).to_broadcast([P // 2, 2, ATOM]),
         )
+        nc.scalar.dma_start(out=adj_sb[:], in_=adj.rearrange("b m (h j) -> (b m h) j", j=TILES))
         nc.scalar.dma_start(out=bonds[:], in_=f_bonds.rearrange("b m (h j) f -> (b m h) j f", j=TILES))
         nc.sync.dma_start(out=weight[:].bitcast(I32), in_=w_words[0].bitcast(I32))
         for q in range(4):
@@ -65,14 +63,12 @@ def tile_mpnencoder_pa_kernel(tc, f_atoms, f_bonds, adj, w_words, w_scales, out)
         adj_f32 = keep.tile([P, TILES], F32, name="adj_f32")
         nc.vector.tensor_copy(out=adj_f32[:], in_=adj_sb[:])
         sorted_atoms = keep.tile([P, PACK, ATOM_K], BF16, name="sorted_atoms")
-        nc.scalar.copy(
-            out=sorted_atoms[:, :, 0 : ATOM // PACK],
-            in_=atoms[:].rearrange("p (k t) -> p t k", t=PACK),
-        )
-        nc.scalar.copy(
-            out=sorted_atoms[:, :, ATOM // PACK : ATOM_K],
-            in_=atoms[:, ATOM - TAIL : ATOM].rearrange("p (k t) -> p t k", t=PACK),
-        )
+        by_t = atoms[:].rearrange("p (k t) -> p t k", t=PACK)
+        tail_by_t = atoms[:, ATOM - TAIL : ATOM].rearrange("p (k t) -> p t k", t=PACK)
+        nc.scalar.copy(out=sorted_atoms[:, 0:2, 0 : ATOM // PACK], in_=by_t[:, 0:2, :])
+        nc.scalar.copy(out=sorted_atoms[:, 0:2, ATOM // PACK : ATOM_K], in_=tail_by_t[:, 0:2, :])
+        nc.vector.tensor_copy(out=sorted_atoms[:, 2:4, 0 : ATOM // PACK], in_=by_t[:, 2:4, :])
+        nc.vector.tensor_copy(out=sorted_atoms[:, 2:4, ATOM // PACK : ATOM_K], in_=tail_by_t[:, 2:4, :])
 
         gated = keep.tile([P, TILES, PACK, P], BF16, name="gated")
         grouped = keep.tile([P, TILES, P, PACK], BF16, name="grouped", align_bytes=64)
@@ -82,79 +78,72 @@ def tile_mpnencoder_pa_kernel(tc, f_atoms, f_bonds, adj, w_words, w_scales, out)
         out_rows = out.rearrange("b m (h j) c -> (b m h) j c", j=TILES)
         flipped = {}
 
-        def gate(first, count):
-            for j in range(first, first + count):
-                nc.vector.tensor_scalar(
-                    out=gated[:, j, :, 0:ATOM_K],
-                    in0=sorted_atoms[:],
-                    scalar1=adj_f32[:, j : j + 1],
-                    scalar2=None,
-                    op0=MULT,
-                )
-                nc.vector.tensor_scalar(
-                    out=gated[:, j, :, ATOM_K:P].rearrange("p t (d k) -> p t d k", d=2),
-                    in0=bonds[:, j, :]
-                    .rearrange("p (k t) -> p t k", t=PACK)
-                    .unsqueeze(2)
-                    .to_broadcast([P, PACK, 2, BOND_K]),
-                    scalar1=adj_f32[:, j : j + 1],
-                    scalar2=None,
-                    op0=MULT,
-                )
-
-        def flip(first, count):
-            bank = flipped_pool.tile([P, count, PACK, P], BF16, name="bank", tag="bank")
-            flipped[first] = bank
-            for i in range(count):
-                for t in range(PACK):
-                    nc.tensor.transpose(bank[:, i, t, :], gated[:, first + i, t, :], identity[:])
-
-        def regroup(first, count):
-            nc.scalar.copy(
-                out=grouped[:, first : first + count, :, :],
-                in_=flipped[first][:].rearrange("k i t p -> k i p t"),
+        def gate(j):
+            nc.vector.tensor_scalar(
+                out=gated[:, j, :, 0:ATOM_K],
+                in0=sorted_atoms[:],
+                scalar1=adj_f32[:, j : j + 1],
+                scalar2=None,
+                op0=MULT,
+            )
+            nc.vector.tensor_scalar(
+                out=gated[:, j, :, ATOM_K:P].rearrange("p t (d k) -> p t d k", d=2),
+                in0=bonds[:, j, :]
+                .rearrange("p (k t) -> p t k", t=PACK)
+                .unsqueeze(2)
+                .to_broadcast([P, PACK, 2, BOND_K]),
+                scalar1=adj_f32[:, j : j + 1],
+                scalar2=None,
+                op0=MULT,
             )
 
-        def quantise(first, count):
+        def flip(j):
+            bank = flipped_pool.tile([P, PACK, P], BF16, name="bank", tag="bank")
+            flipped[j] = bank
+            for t in range(PACK):
+                nc.tensor.transpose(bank[:, t, :], gated[:, j, t, :], identity[:])
+
+        def regroup(j):
+            nc.scalar.copy(out=grouped[:, j, :, :], in_=flipped[j][:].rearrange("k t p -> k p t"))
+
+        def quantise(j):
             nc.vector.quantize_mx(
-                out=codes[:, first : first + count, :].rearrange("k i p -> k (i p)").bitcast(FP8X4),
-                scales=scales[:, first : first + count, :].rearrange("k i p -> k (i p)"),
-                in_=grouped[:, first : first + count, :, :].rearrange("k i p t -> k (i p t)"),
+                out=codes[:, j, :].bitcast(FP8X4),
+                scales=scales[:, j, :],
+                in_=grouped[:, j, :, :].rearrange("k p t -> k (p t)"),
             )
 
-        def project(first, count):
-            for j in range(first, first + count):
-                for half in range(HIDDEN // BANK):
-                    acc = acc_pool.tile([P, BANK], F32, name="acc", tag="acc")
-                    nc.tensor.matmul_mx(
-                        out=acc[:],
-                        lhsT=codes[:, j, :].bitcast(FP8X4),
-                        lhsT_scale=scales[:, j, :],
-                        rhs=weight[:, 2 * BANK * half : 2 * BANK * (half + 1)].bitcast(FP4X4),
-                        rhs_scale=weight_scales[:, BANK * half : BANK * (half + 1)],
-                        start=True,
-                        stop=True,
-                    )
-                    columns = result[:, j, BANK * half : BANK * (half + 1)]
-                    if half == 0:
-                        nc.vector.tensor_copy(out=columns, in_=acc[:])
-                    else:
-                        nc.scalar.copy(out=columns, in_=acc[:])
-                nc.sync.dma_start(out=out_rows[:, j, :], in_=result[:, j, :])
+        def project(j):
+            for half in range(HIDDEN // BANK):
+                acc = acc_pool.tile([P, BANK], F32, name="acc", tag="acc")
+                nc.tensor.matmul_mx(
+                    out=acc[:],
+                    lhsT=codes[:, j, :].bitcast(FP8X4),
+                    lhsT_scale=scales[:, j, :],
+                    rhs=weight[:, 2 * BANK * half : 2 * BANK * (half + 1)].bitcast(FP4X4),
+                    rhs_scale=weight_scales[:, BANK * half : BANK * (half + 1)],
+                    start=True,
+                    stop=True,
+                )
+                columns = result[:, j, BANK * half : BANK * (half + 1)]
+                if half == 0:
+                    nc.vector.tensor_copy(out=columns, in_=acc[:])
+                else:
+                    nc.scalar.copy(out=columns, in_=acc[:])
+            nc.sync.dma_start(out=out_rows[:, j, :], in_=result[:, j, :])
 
-        n = len(groups)
-        for i in range(3):
-            gate(*groups[i])
-        for i in range(2):
-            flip(*groups[i])
-            regroup(*groups[i])
-        quantise(*groups[0])
-        for i in range(n):
-            if i + 3 < n:
-                gate(*groups[i + 3])
-            if i + 2 < n:
-                flip(*groups[i + 2])
-                regroup(*groups[i + 2])
-            if i + 1 < n:
-                quantise(*groups[i + 1])
-            project(*groups[i])
+        for j in range(3):
+            gate(j)
+        for j in range(2):
+            flip(j)
+            regroup(j)
+        quantise(0)
+        for j in range(TILES):
+            if j + 3 < TILES:
+                gate(j + 3)
+            if j + 2 < TILES:
+                flip(j + 2)
+                regroup(j + 2)
+            if j + 1 < TILES:
+                quantise(j + 1)
+            project(j)

@@ -23,6 +23,9 @@ ATOM_K = (ATOM + TAIL) // PACK
 BOND_K = BOND // PACK
 HIDDEN = 1024
 BANK = 512
+SHARE = 4
+WARM_FIRST = 3
+WARM_STEP = 2
 
 FLOPS = 2 * PAIRS * 512 * HIDDEN
 
@@ -44,12 +47,22 @@ def tile_mpnencoder_pa_kernel(tc, f_atoms, f_bonds, adj, w_words, w_scales, out)
 
         nc.vector.memset(weight_scales[:].bitcast(I32), 0)
 
+        zeros = keep.tile([P, BANK], BF16, name="zeros")
+        nc.vector.memset(zeros[:], 0.0)
+        idle_sums = acc_pool.tile([P, BANK], F32, name="idle_sums", tag="acc")
+
+        def keep_warm(count):
+            for i in range(count):
+                nc.tensor.matmul(out=idle_sums[:], lhsT=zeros[:, 0:P], rhs=zeros[:], start=True, stop=True)
+
+        keep_warm(WARM_FIRST)
+
         nc.sync.dma_start(
             out=atoms[:],
             in_=f_atoms.rearrange("b m f -> (b m) f").unsqueeze(1).to_broadcast([P // 2, 2, ATOM]),
         )
-        nc.scalar.dma_start(out=adj_sb[:], in_=adj.rearrange("b m (h j) -> (b m h) j", j=TILES))
-        nc.scalar.dma_start(out=bonds[:], in_=f_bonds.rearrange("b m (h j) f -> (b m h) j f", j=TILES))
+        nc.sync.dma_start(out=adj_sb[:], in_=adj.rearrange("b m (h j) -> (b m h) j", j=TILES))
+        nc.sync.dma_start(out=bonds[:], in_=f_bonds.rearrange("b m (h j) f -> (b m h) j f", j=TILES))
         nc.sync.dma_start(out=weight[:].bitcast(I32), in_=w_words[0].bitcast(I32))
         for q in range(4):
             nc.sync.dma_start(
@@ -60,8 +73,6 @@ def tile_mpnencoder_pa_kernel(tc, f_atoms, f_bonds, adj, w_words, w_scales, out)
         identity = keep.tile([P, P], BF16, name="identity")
         make_identity(nc, identity[:])
 
-        adj_f32 = keep.tile([P, TILES], F32, name="adj_f32")
-        nc.vector.tensor_copy(out=adj_f32[:], in_=adj_sb[:])
         sorted_atoms = keep.tile([P, PACK, ATOM_K], BF16, name="sorted_atoms")
         by_t = atoms[:].rearrange("p (k t) -> p t k", t=PACK)
         tail_by_t = atoms[:, ATOM - TAIL : ATOM].rearrange("p (k t) -> p t k", t=PACK)
@@ -82,7 +93,7 @@ def tile_mpnencoder_pa_kernel(tc, f_atoms, f_bonds, adj, w_words, w_scales, out)
             nc.vector.tensor_scalar(
                 out=gated[:, j, :, 0:ATOM_K],
                 in0=sorted_atoms[:],
-                scalar1=adj_f32[:, j : j + 1],
+                scalar1=adj_sb[:, j : j + 1],
                 scalar2=None,
                 op0=MULT,
             )
@@ -92,7 +103,7 @@ def tile_mpnencoder_pa_kernel(tc, f_atoms, f_bonds, adj, w_words, w_scales, out)
                 .rearrange("p (k t) -> p t k", t=PACK)
                 .unsqueeze(2)
                 .to_broadcast([P, PACK, 2, BOND_K]),
-                scalar1=adj_f32[:, j : j + 1],
+                scalar1=adj_sb[:, j : j + 1],
                 scalar2=None,
                 op0=MULT,
             )
@@ -126,16 +137,20 @@ def tile_mpnencoder_pa_kernel(tc, f_atoms, f_bonds, adj, w_words, w_scales, out)
                     stop=True,
                 )
                 columns = result[:, j, BANK * half : BANK * (half + 1)]
-                if half == 0:
+                if half == 0 or j % SHARE == 1:
                     nc.vector.tensor_copy(out=columns, in_=acc[:])
                 else:
                     nc.scalar.copy(out=columns, in_=acc[:])
-            nc.sync.dma_start(out=out_rows[:, j, :], in_=result[:, j, :])
+                if j == 0:
+                    nc.sync.dma_start(out=out_rows[:, j, BANK * half : BANK * (half + 1)], in_=columns)
+            if j > 0:
+                nc.sync.dma_start(out=out_rows[:, j, :], in_=result[:, j, :])
 
         for j in range(3):
             gate(j)
         for j in range(2):
             flip(j)
+            keep_warm(WARM_STEP)
             regroup(j)
         quantise(0)
         for j in range(TILES):

@@ -13,21 +13,20 @@ FP4X4 = mybir.dt.float4_e2m1fn_x4
 MULT = mybir.AluOpType.mult
 
 P = 128
-PACK = 4
 PAIRS = 2 * 32 * 32
 TILES = PAIRS // P
 ATOM = 352
 TAIL = 96
 BOND = 32
-ATOM_K = (ATOM + TAIL) // PACK
-BOND_K = BOND // PACK
+ATOMS = ATOM + TAIL
+FEATURES = ATOMS + 2 * BOND
+HALVES = 2
 HIDDEN = 1024
 BANK = 512
-SHARE = 4
 WARM_FIRST = 3
 WARM_STEP = 2
 
-FLOPS = 2 * PAIRS * 512 * HIDDEN
+FLOPS = 2 * PAIRS * FEATURES * HIDDEN
 
 
 def tile_mpnencoder_pa_kernel(tc, f_atoms, f_bonds, adj, w_words, w_scales, out):
@@ -40,7 +39,7 @@ def tile_mpnencoder_pa_kernel(tc, f_atoms, f_bonds, adj, w_words, w_scales, out)
         ctx.enter_context(tc.manual_schedule())
 
         adj_sb = keep.tile([P, TILES], BF16, name="adj_sb")
-        atoms = keep.tile([P, ATOM], BF16, name="atoms")
+        atoms = keep.tile([P, ATOMS], BF16, name="atoms")
         bonds = keep.tile([P, TILES, BOND], BF16, name="bonds")
         weight = keep.tile([P, 2 * HIDDEN], U8, name="weight", align_bytes=64)
         weight_scales = keep.tile([P, HIDDEN], U8, name="weight_scales", align_bytes=64)
@@ -57,9 +56,13 @@ def tile_mpnencoder_pa_kernel(tc, f_atoms, f_bonds, adj, w_words, w_scales, out)
 
         keep_warm(WARM_FIRST)
 
+        atom_rows = f_atoms.rearrange("b m f -> (b m) f")
         nc.sync.dma_start(
-            out=atoms[:],
-            in_=f_atoms.rearrange("b m f -> (b m) f").unsqueeze(1).to_broadcast([P // 2, 2, ATOM]),
+            out=atoms[:, 0:ATOM], in_=atom_rows.unsqueeze(1).to_broadcast([P // 2, 2, ATOM])
+        )
+        nc.sync.dma_start(
+            out=atoms[:, ATOM:ATOMS],
+            in_=atom_rows[:, ATOM - TAIL : ATOM].unsqueeze(1).to_broadcast([P // 2, 2, TAIL]),
         )
         nc.sync.dma_start(out=adj_sb[:], in_=adj.rearrange("b m (h j) -> (b m h) j", j=TILES))
         nc.sync.dma_start(out=bonds[:], in_=f_bonds.rearrange("b m (h j) f -> (b m h) j f", j=TILES))
@@ -70,19 +73,11 @@ def tile_mpnencoder_pa_kernel(tc, f_atoms, f_bonds, adj, w_words, w_scales, out)
                 in_=w_scales[0, 4 * q : 4 * q + 4, :].bitcast(I32),
             )
 
-        identity = keep.tile([P, P], BF16, name="identity")
+        identity = keep.tile([P, P], F32, name="identity")
         make_identity(nc, identity[:])
 
-        sorted_atoms = keep.tile([P, PACK, ATOM_K], BF16, name="sorted_atoms")
-        by_t = atoms[:].rearrange("p (k t) -> p t k", t=PACK)
-        tail_by_t = atoms[:, ATOM - TAIL : ATOM].rearrange("p (k t) -> p t k", t=PACK)
-        nc.scalar.copy(out=sorted_atoms[:, 0:2, 0 : ATOM // PACK], in_=by_t[:, 0:2, :])
-        nc.scalar.copy(out=sorted_atoms[:, 0:2, ATOM // PACK : ATOM_K], in_=tail_by_t[:, 0:2, :])
-        nc.vector.tensor_copy(out=sorted_atoms[:, 2:4, 0 : ATOM // PACK], in_=by_t[:, 2:4, :])
-        nc.vector.tensor_copy(out=sorted_atoms[:, 2:4, ATOM // PACK : ATOM_K], in_=tail_by_t[:, 2:4, :])
-
-        gated = keep.tile([P, TILES, PACK, P], BF16, name="gated")
-        grouped = keep.tile([P, TILES, P, PACK], BF16, name="grouped", align_bytes=64)
+        gated = keep.tile([P, TILES, FEATURES], BF16, name="gated")
+        grouped = keep.tile([P, TILES, PAIRS // TILES * 4], BF16, name="grouped", align_bytes=64)
         codes = keep.tile([P, TILES, P], U32, name="codes", align_bytes=64)
         scales = keep.tile([P, TILES, P], U8, name="scales", align_bytes=64)
         result = keep.tile([P, TILES, HIDDEN], F32, name="result")
@@ -91,37 +86,38 @@ def tile_mpnencoder_pa_kernel(tc, f_atoms, f_bonds, adj, w_words, w_scales, out)
 
         def gate(j):
             nc.vector.tensor_scalar(
-                out=gated[:, j, :, 0:ATOM_K],
-                in0=sorted_atoms[:],
+                out=gated[:, j, 0:ATOMS],
+                in0=atoms[:],
                 scalar1=adj_sb[:, j : j + 1],
                 scalar2=None,
                 op0=MULT,
             )
             nc.vector.tensor_scalar(
-                out=gated[:, j, :, ATOM_K:P].rearrange("p t (d k) -> p t d k", d=2),
-                in0=bonds[:, j, :]
-                .rearrange("p (k t) -> p t k", t=PACK)
-                .unsqueeze(2)
-                .to_broadcast([P, PACK, 2, BOND_K]),
+                out=gated[:, j, ATOMS:FEATURES].rearrange("p (d f) -> p d f", d=2),
+                in0=bonds[:, j, :].unsqueeze(1).to_broadcast([P, 2, BOND]),
                 scalar1=adj_sb[:, j : j + 1],
                 scalar2=None,
                 op0=MULT,
             )
 
         def flip(j):
-            bank = flipped_pool.tile([P, PACK, P], BF16, name="bank", tag="bank")
+            bank = flipped_pool.tile([P, BANK], F32, name="bank", tag="bank")
             flipped[j] = bank
-            for t in range(PACK):
-                nc.tensor.transpose(bank[:, t, :], gated[:, j, t, :], identity[:])
+            words = gated[:, j, :].bitcast(F32)
+            for u in range(HALVES):
+                nc.tensor.transpose(bank[:, u * P : (u + 1) * P], words[:, u : FEATURES // 2 : HALVES], identity[:])
 
         def regroup(j):
-            nc.scalar.copy(out=grouped[:, j, :, :], in_=flipped[j][:].rearrange("k t p -> k p t"))
+            nc.scalar.copy(
+                out=grouped[:, j, :].bitcast(F32).rearrange("k (p u) -> k p u", u=HALVES),
+                in_=flipped[j][:, 0 : HALVES * P].rearrange("k (u p) -> k p u", u=HALVES),
+            )
 
         def quantise(j):
             nc.vector.quantize_mx(
                 out=codes[:, j, :].bitcast(FP8X4),
                 scales=scales[:, j, :],
-                in_=grouped[:, j, :, :].rearrange("k p t -> k (p t)"),
+                in_=grouped[:, j, :],
             )
 
         def project(j):
@@ -137,7 +133,7 @@ def tile_mpnencoder_pa_kernel(tc, f_atoms, f_bonds, adj, w_words, w_scales, out)
                     stop=True,
                 )
                 columns = result[:, j, BANK * half : BANK * (half + 1)]
-                if half == 0 or j % SHARE == 1:
+                if half == 0:
                     nc.vector.tensor_copy(out=columns, in_=acc[:])
                 else:
                     nc.scalar.copy(out=columns, in_=acc[:])

@@ -23,6 +23,8 @@ FEATURES = ATOMS + 2 * BOND
 HALVES = 2
 HIDDEN = 1024
 BANK = 512
+PIECES = {0: BANK // 2, 1: BANK}
+JOIN_FROM = TILES
 WARM_FIRST = 3
 WARM_STEP = 2
 
@@ -60,10 +62,6 @@ def tile_mpnencoder_pa_kernel(tc, f_atoms, f_bonds, adj, w_words, w_scales, out)
         nc.sync.dma_start(
             out=atoms[:, 0:ATOM], in_=atom_rows.unsqueeze(1).to_broadcast([P // 2, 2, ATOM])
         )
-        nc.sync.dma_start(
-            out=atoms[:, ATOM:ATOMS],
-            in_=atom_rows[:, ATOM - TAIL : ATOM].unsqueeze(1).to_broadcast([P // 2, 2, TAIL]),
-        )
         nc.sync.dma_start(out=adj_sb[:], in_=adj.rearrange("b m (h j) -> (b m h) j", j=TILES))
         nc.sync.dma_start(out=bonds[:], in_=f_bonds.rearrange("b m (h j) f -> (b m h) j f", j=TILES))
         nc.sync.dma_start(out=weight[:].bitcast(I32), in_=w_words[0].bitcast(I32))
@@ -84,14 +82,33 @@ def tile_mpnencoder_pa_kernel(tc, f_atoms, f_bonds, adj, w_words, w_scales, out)
         out_rows = out.rearrange("b m (h j) c -> (b m h) j c", j=TILES)
         flipped = {}
 
+        def repeat_tail():
+            nc.scalar.copy(out=atoms[:, ATOM:ATOMS], in_=atoms[:, ATOM - TAIL : ATOM])
+
         def gate(j):
-            nc.vector.tensor_scalar(
-                out=gated[:, j, 0:ATOMS],
-                in0=atoms[:],
-                scalar1=adj_sb[:, j : j + 1],
-                scalar2=None,
-                op0=MULT,
-            )
+            if j == 0:
+                nc.vector.tensor_scalar(
+                    out=gated[:, j, 0:ATOM],
+                    in0=atoms[:, 0:ATOM],
+                    scalar1=adj_sb[:, j : j + 1],
+                    scalar2=None,
+                    op0=MULT,
+                )
+                nc.vector.tensor_scalar(
+                    out=gated[:, j, ATOM:ATOMS],
+                    in0=atoms[:, ATOM - TAIL : ATOM],
+                    scalar1=adj_sb[:, j : j + 1],
+                    scalar2=None,
+                    op0=MULT,
+                )
+            else:
+                nc.vector.tensor_scalar(
+                    out=gated[:, j, 0:ATOMS],
+                    in0=atoms[:],
+                    scalar1=adj_sb[:, j : j + 1],
+                    scalar2=None,
+                    op0=MULT,
+                )
             nc.vector.tensor_scalar(
                 out=gated[:, j, ATOMS:FEATURES].rearrange("p (d f) -> p d f", d=2),
                 in0=bonds[:, j, :].unsqueeze(1).to_broadcast([P, 2, BOND]),
@@ -121,27 +138,34 @@ def tile_mpnencoder_pa_kernel(tc, f_atoms, f_bonds, adj, w_words, w_scales, out)
             )
 
         def project(j):
-            for half in range(HIDDEN // BANK):
+            width = PIECES.get(j, BANK)
+            for piece in range(HIDDEN // width):
                 acc = acc_pool.tile([P, BANK], F32, name="acc", tag="acc")
+                first = piece * width
                 nc.tensor.matmul_mx(
-                    out=acc[:],
+                    out=acc[:, 0:width],
                     lhsT=codes[:, j, :].bitcast(FP8X4),
                     lhsT_scale=scales[:, j, :],
-                    rhs=weight[:, 2 * BANK * half : 2 * BANK * (half + 1)].bitcast(FP4X4),
-                    rhs_scale=weight_scales[:, BANK * half : BANK * (half + 1)],
+                    rhs=weight[:, 2 * first : 2 * (first + width)].bitcast(FP4X4),
+                    rhs_scale=weight_scales[:, first : first + width],
                     start=True,
                     stop=True,
                 )
-                columns = result[:, j, BANK * half : BANK * (half + 1)]
-                if half == 0:
-                    nc.vector.tensor_copy(out=columns, in_=acc[:])
+                columns = result[:, j, first : first + width]
+                if piece % 2 == 0:
+                    nc.vector.tensor_copy(out=columns, in_=acc[:, 0:width])
                 else:
-                    nc.scalar.copy(out=columns, in_=acc[:])
-                if j == 0:
-                    nc.sync.dma_start(out=out_rows[:, j, BANK * half : BANK * (half + 1)], in_=columns)
-            if j > 0:
+                    nc.scalar.copy(out=columns, in_=acc[:, 0:width])
+                if j in PIECES:
+                    nc.sync.dma_start(out=out_rows[:, j, first : first + width], in_=columns)
+            if j in PIECES:
+                return
+            if j < JOIN_FROM:
                 nc.sync.dma_start(out=out_rows[:, j, :], in_=result[:, j, :])
+            elif (j - JOIN_FROM) % 2 == 1:
+                nc.sync.dma_start(out=out_rows[:, j - 1 : j + 1, :], in_=result[:, j - 1 : j + 1, :])
 
+        repeat_tail()
         for j in range(3):
             gate(j)
         for j in range(2):

@@ -25,7 +25,7 @@ HIDDEN = 1024
 BANK = 512
 PIECES = {0: BANK // 2, 1: BANK}
 JOIN_FROM = TILES
-WARM_FIRST = 3
+WARM_FIRST = 4
 WARM_STEP = 2
 
 FLOPS = 2 * PAIRS * FEATURES * HIDDEN
@@ -46,10 +46,9 @@ def tile_mpnencoder_pa_kernel(tc, f_atoms, f_bonds, adj, w_words, w_scales, out)
         weight = keep.tile([P, 2 * HIDDEN], U8, name="weight", align_bytes=64)
         weight_scales = keep.tile([P, HIDDEN], U8, name="weight_scales", align_bytes=64)
 
-        nc.vector.memset(weight_scales[:].bitcast(I32), 0)
-
         zeros = keep.tile([P, BANK], BF16, name="zeros")
-        nc.vector.memset(zeros[:], 0.0)
+        nc.vector.memset(zeros[:].bitcast(I32), 0)
+        nc.vector.memset(weight_scales[:].bitcast(I32), 0)
         idle_sums = acc_pool.tile([P, BANK], F32, name="idle_sums", tag="acc")
 
         def keep_warm(count):

@@ -25,6 +25,7 @@ HIDDEN = 1024
 BANK = 512
 PIECES = {0: BANK // 2, 1: BANK}
 JOIN_FROM = TILES
+BONDS_FIRST = 4
 WARM_FIRST = 4
 WARM_STEP = 2
 
@@ -62,13 +63,15 @@ def tile_mpnencoder_pa_kernel(tc, f_atoms, f_bonds, adj, w_words, w_scales, out)
             out=atoms[:, 0:ATOM], in_=atom_rows.unsqueeze(1).to_broadcast([P // 2, 2, ATOM])
         )
         nc.sync.dma_start(out=adj_sb[:], in_=adj.rearrange("b m (h j) -> (b m h) j", j=TILES))
-        nc.sync.dma_start(out=bonds[:], in_=f_bonds.rearrange("b m (h j) f -> (b m h) j f", j=TILES))
+        bond_rows = f_bonds.rearrange("b m (h j) f -> (b m h) j f", j=TILES)
+        nc.sync.dma_start(out=bonds[:, 0:BONDS_FIRST, :], in_=bond_rows[:, 0:BONDS_FIRST, :])
         nc.sync.dma_start(out=weight[:].bitcast(I32), in_=w_words[0].bitcast(I32))
         for q in range(4):
             nc.sync.dma_start(
                 out=weight_scales[32 * q : 32 * q + 4, :].bitcast(I32),
                 in_=w_scales[0, 4 * q : 4 * q + 4, :].bitcast(I32),
             )
+        nc.sync.dma_start(out=bonds[:, BONDS_FIRST:TILES, :], in_=bond_rows[:, BONDS_FIRST:TILES, :])
 
         identity = keep.tile([P, P], F32, name="identity")
         make_identity(nc, identity[:])

@@ -26,7 +26,7 @@ BANK = 512
 PIECES = {0: BANK // 2, 1: BANK}
 JOIN_FROM = TILES
 BONDS_FIRST = 4
-WARM_FIRST = 4
+WARM_FIRST = 5
 WARM_STEP = 2
 
 FLOPS = 2 * PAIRS * FEATURES * HIDDEN
@@ -47,14 +47,20 @@ def tile_mpnencoder_pa_kernel(tc, f_atoms, f_bonds, adj, w_words, w_scales, out)
         weight = keep.tile([P, 2 * HIDDEN], U8, name="weight", align_bytes=64)
         weight_scales = keep.tile([P, HIDDEN], U8, name="weight_scales", align_bytes=64)
 
-        zeros = keep.tile([P, BANK], BF16, name="zeros")
-        nc.vector.memset(zeros[:].bitcast(I32), 0)
+        zeros = keep.tile([P, 2], BF16, name="zeros")
+        nc.gpsimd.memset(zeros[:].bitcast(I32), 0)
         nc.vector.memset(weight_scales[:].bitcast(I32), 0)
         idle_sums = acc_pool.tile([P, BANK], F32, name="idle_sums", tag="acc")
 
         def keep_warm(count):
             for i in range(count):
-                nc.tensor.matmul(out=idle_sums[:], lhsT=zeros[:, 0:P], rhs=zeros[:], start=True, stop=True)
+                nc.tensor.matmul(
+                    out=idle_sums[:],
+                    lhsT=zeros[:, 0:1].to_broadcast([P, P]),
+                    rhs=zeros[:, 0:1].to_broadcast([P, BANK]),
+                    start=True,
+                    stop=True,
+                )
 
         keep_warm(WARM_FIRST)
 

@@ -25,9 +25,10 @@ HIDDEN = 1024
 BANK = 512
 PIECES = {0: BANK // 2, 1: BANK}
 JOIN_FROM = TILES
-BONDS_FIRST = 4
-WARM_FIRST = 5
-WARM_STEP = 2
+BONDS_FIRST = 8
+GATES_FIRST = 5
+WARM_FIRST = 9
+WARM_SECOND = 5
 
 FLOPS = 2 * PAIRS * FEATURES * HIDDEN
 
@@ -37,13 +38,15 @@ def tile_mpnencoder_pa_kernel(tc, f_atoms, f_bonds, adj, w_words, w_scales, out)
 
     with ExitStack() as ctx:
         keep = ctx.enter_context(tc.tile_pool(name="keep", bufs=1))
-        flipped_pool = ctx.enter_context(tc.psum_pool(name="flipped", bufs=2))
-        acc_pool = ctx.enter_context(tc.psum_pool(name="acc", bufs=6))
+        flipped_pool = ctx.enter_context(tc.psum_pool(name="flipped", bufs=3))
+        acc_pool = ctx.enter_context(tc.psum_pool(name="acc", bufs=5))
         ctx.enter_context(tc.manual_schedule())
 
         adj_sb = keep.tile([P, TILES], BF16, name="adj_sb")
-        atoms = keep.tile([P, ATOMS], BF16, name="atoms")
+        atoms = keep.tile([P, ATOM], BF16, name="atoms")
         bonds = keep.tile([P, TILES, BOND], BF16, name="bonds")
+        halved_atoms = keep.tile([P, HALVES, ATOMS // HALVES], BF16, name="halved_atoms")
+        halved_bonds = keep.tile([P, TILES, HALVES, BOND // HALVES], BF16, name="halved_bonds")
         weight = keep.tile([P, 2 * HIDDEN], U8, name="weight", align_bytes=64)
         weight_scales = keep.tile([P, HIDDEN], U8, name="weight_scales", align_bytes=64)
 
@@ -55,9 +58,9 @@ def tile_mpnencoder_pa_kernel(tc, f_atoms, f_bonds, adj, w_words, w_scales, out)
         def keep_warm(count):
             for i in range(count):
                 nc.tensor.matmul(
-                    out=idle_sums[:],
+                    out=idle_sums[:, 0 : BANK // 2],
                     lhsT=zeros[:, 0:1].to_broadcast([P, P]),
-                    rhs=zeros[:, 0:1].to_broadcast([P, BANK]),
+                    rhs=zeros[:, 0:1].to_broadcast([P, BANK // 2]),
                     start=True,
                     stop=True,
                 )
@@ -66,7 +69,7 @@ def tile_mpnencoder_pa_kernel(tc, f_atoms, f_bonds, adj, w_words, w_scales, out)
 
         atom_rows = f_atoms.rearrange("b m f -> (b m) f")
         nc.sync.dma_start(
-            out=atoms[:, 0:ATOM], in_=atom_rows.unsqueeze(1).to_broadcast([P // 2, 2, ATOM])
+            out=atoms[:], in_=atom_rows.unsqueeze(1).to_broadcast([P // 2, 2, ATOM])
         )
         nc.sync.dma_start(out=adj_sb[:], in_=adj.rearrange("b m (h j) -> (b m h) j", j=TILES))
         bond_rows = f_bonds.rearrange("b m (h j) f -> (b m h) j f", j=TILES)
@@ -86,56 +89,57 @@ def tile_mpnencoder_pa_kernel(tc, f_atoms, f_bonds, adj, w_words, w_scales, out)
         grouped = keep.tile([P, TILES, PAIRS // TILES * 4], BF16, name="grouped", align_bytes=64)
         codes = keep.tile([P, TILES, P], U32, name="codes", align_bytes=64)
         scales = keep.tile([P, TILES, P], U8, name="scales", align_bytes=64)
-        result = keep.tile([P, TILES, HIDDEN], F32, name="result")
+        result = keep.tile([P, TILES, HIDDEN], F32, name="result", align_bytes=256)
         out_rows = out.rearrange("b m (h j) c -> (b m h) j c", j=TILES)
         flipped = {}
 
-        def repeat_tail():
-            nc.scalar.copy(out=atoms[:, ATOM:ATOMS], in_=atoms[:, ATOM - TAIL : ATOM])
+        def halve_atoms():
+            halved = halved_atoms[:].bitcast(F32)
+            words = atoms[:].bitcast(F32).rearrange("p (w u) -> p u w", u=HALVES)
+            first = ATOM // 4
+            nc.scalar.copy(out=halved[:, :, 0:first], in_=words)
+            nc.scalar.copy(out=halved[:, :, first:], in_=words[:, :, first - TAIL // 4 : first])
 
-        def gate(j):
-            if j == 0:
-                nc.vector.tensor_scalar(
-                    out=gated[:, j, 0:ATOM],
-                    in0=atoms[:, 0:ATOM],
-                    scalar1=adj_sb[:, j : j + 1],
-                    scalar2=None,
-                    op0=MULT,
-                )
-                nc.vector.tensor_scalar(
-                    out=gated[:, j, ATOM:ATOMS],
-                    in0=atoms[:, ATOM - TAIL : ATOM],
-                    scalar1=adj_sb[:, j : j + 1],
-                    scalar2=None,
-                    op0=MULT,
-                )
-            else:
-                nc.vector.tensor_scalar(
-                    out=gated[:, j, 0:ATOMS],
-                    in0=atoms[:],
-                    scalar1=adj_sb[:, j : j + 1],
-                    scalar2=None,
-                    op0=MULT,
-                )
-            nc.vector.tensor_scalar(
-                out=gated[:, j, ATOMS:FEATURES].rearrange("p (d f) -> p d f", d=2),
-                in0=bonds[:, j, :].unsqueeze(1).to_broadcast([P, 2, BOND]),
-                scalar1=adj_sb[:, j : j + 1],
-                scalar2=None,
-                op0=MULT,
+        def halve_bonds(begin, end):
+            nc.scalar.copy(
+                out=halved_bonds[:, begin:end].bitcast(F32),
+                in_=bonds[:, begin:end].bitcast(F32).rearrange("p j (w u) -> p j u w", u=HALVES),
             )
 
-        def flip(j):
+        def gate(j):
+            weight_of_pair = adj_sb[:, j : j + 1]
+
+            def times(out, features):
+                nc.vector.tensor_scalar(out=out, in0=features, scalar1=weight_of_pair, scalar2=None, op0=MULT)
+
+            if j == 0:
+                times(gated[:, j, 0:ATOM], atoms[:])
+                times(gated[:, j, ATOM:ATOMS], atoms[:, ATOM - TAIL : ATOM])
+                times(
+                    gated[:, j, ATOMS:FEATURES].rearrange("p (d f) -> p d f", d=2),
+                    bonds[:, j, :].unsqueeze(1).to_broadcast([P, 2, BOND]),
+                )
+            else:
+                halves = gated[:, j, :].rearrange("p (u f) -> p u f", u=HALVES)
+                times(halves[:, :, 0 : ATOMS // HALVES], halved_atoms[:])
+                times(
+                    halves[:, :, ATOMS // HALVES :].rearrange("p u (d f) -> p u d f", d=2),
+                    halved_bonds[:, j].unsqueeze(2).to_broadcast([P, HALVES, 2, BOND // HALVES]),
+                )
+
+        def flip(*tiles):
             bank = flipped_pool.tile([P, BANK], F32, name="bank", tag="bank")
-            flipped[j] = bank
-            words = gated[:, j, :].bitcast(F32)
-            for u in range(HALVES):
-                nc.tensor.transpose(bank[:, u * P : (u + 1) * P], words[:, u : FEATURES // 2 : HALVES], identity[:])
+            for i, j in enumerate(tiles):
+                flipped[j] = bank[:, i * HALVES * P : (i + 1) * HALVES * P]
+                words = gated[:, j, :].bitcast(F32)
+                for u in range(HALVES):
+                    half = words[:, u : FEATURES // 2 : HALVES] if j == 0 else words[:, u * P : (u + 1) * P]
+                    nc.tensor.transpose(flipped[j][:, u * P : (u + 1) * P], half, identity[:])
 
         def regroup(j):
             nc.scalar.copy(
                 out=grouped[:, j, :].bitcast(F32).rearrange("k (p u) -> k p u", u=HALVES),
-                in_=flipped[j][:, 0 : HALVES * P].rearrange("k (u p) -> k p u", u=HALVES),
+                in_=flipped[j].rearrange("k (u p) -> k p u", u=HALVES),
             )
 
         def quantise(j):
@@ -173,20 +177,31 @@ def tile_mpnencoder_pa_kernel(tc, f_atoms, f_bonds, adj, w_words, w_scales, out)
             elif (j - JOIN_FROM) % 2 == 1:
                 nc.sync.dma_start(out=out_rows[:, j - 1 : j + 1, :], in_=result[:, j - 1 : j + 1, :])
 
-        repeat_tail()
-        for j in range(3):
+        halve_atoms()
+        halve_bonds(1, BONDS_FIRST)
+        for j in range(GATES_FIRST):
             gate(j)
-        for j in range(2):
-            flip(j)
-            keep_warm(WARM_STEP)
-            regroup(j)
+        flip(0)
+        regroup(0)
+        flip(1, 2)
+        regroup(1)
+        regroup(2)
+        flip(3)
+        regroup(3)
+        keep_warm(WARM_SECOND)
         quantise(0)
+        quantise(1)
         for j in range(TILES):
-            if j + 3 < TILES:
-                gate(j + 3)
-            if j + 2 < TILES:
-                flip(j + 2)
-                regroup(j + 2)
-            if j + 1 < TILES:
-                quantise(j + 1)
             project(j)
+            if j == 0:
+                quantise(2)
+                continue
+            if j + 3 < TILES:
+                flip(j + 3)
+                regroup(j + 3)
+            if j + 2 < TILES:
+                quantise(j + 2)
+            if j + 4 < TILES:
+                gate(j + 4)
+            if j == 2:
+                halve_bonds(BONDS_FIRST, TILES)

@@ -23,12 +23,17 @@ FEATURES = ATOMS + 2 * BOND
 HALVES = 2
 HIDDEN = 1024
 BANK = 512
-PIECES = {0: BANK // 2, 1: BANK}
-JOIN_FROM = TILES
+HALF = BANK // 2
+PIECES = {
+    0: ((HALF // 2, True), (HALF // 2, True), (HALF, False), (HALF, True), (HALF, False)),
+    1: ((HALF, True), (HALF, False), (HALF, True), (HALF, False)),
+}
+WHOLE_BANKS = ((BANK, True), (BANK, False))
+STORES = {0: (1, 1, 1, 2), 1: (2, 2)}
 BONDS_FIRST = 8
-GATES_FIRST = 5
+GATES_FIRST = 6
 WARM_FIRST = 9
-WARM_SECOND = 5
+WARM_SECOND = 4
 
 FLOPS = 2 * PAIRS * FEATURES * HIDDEN
 
@@ -38,8 +43,7 @@ def tile_mpnencoder_pa_kernel(tc, f_atoms, f_bonds, adj, w_words, w_scales, out)
 
     with ExitStack() as ctx:
         keep = ctx.enter_context(tc.tile_pool(name="keep", bufs=1))
-        flipped_pool = ctx.enter_context(tc.psum_pool(name="flipped", bufs=3))
-        acc_pool = ctx.enter_context(tc.psum_pool(name="acc", bufs=5))
+        banks = ctx.enter_context(tc.psum_pool(name="banks", bufs=8))
         ctx.enter_context(tc.manual_schedule())
 
         adj_sb = keep.tile([P, TILES], BF16, name="adj_sb")
@@ -53,7 +57,7 @@ def tile_mpnencoder_pa_kernel(tc, f_atoms, f_bonds, adj, w_words, w_scales, out)
         zeros = keep.tile([P, 2], BF16, name="zeros")
         nc.gpsimd.memset(zeros[:].bitcast(I32), 0)
         nc.vector.memset(weight_scales[:].bitcast(I32), 0)
-        idle_sums = acc_pool.tile([P, BANK], F32, name="idle_sums", tag="acc")
+        idle_sums = banks.tile([P, BANK], F32, name="idle_sums", tag="bank")
 
         def keep_warm(count):
             for i in range(count):
@@ -128,7 +132,7 @@ def tile_mpnencoder_pa_kernel(tc, f_atoms, f_bonds, adj, w_words, w_scales, out)
                 )
 
         def flip(*tiles):
-            bank = flipped_pool.tile([P, BANK], F32, name="bank", tag="bank")
+            bank = banks.tile([P, BANK], F32, name="bank", tag="bank")
             for i, j in enumerate(tiles):
                 flipped[j] = bank[:, i * HALVES * P : (i + 1) * HALVES * P]
                 words = gated[:, j, :].bitcast(F32)
@@ -150,10 +154,11 @@ def tile_mpnencoder_pa_kernel(tc, f_atoms, f_bonds, adj, w_words, w_scales, out)
             )
 
         def project(j):
-            width = PIECES.get(j, BANK)
-            for piece in range(HIDDEN // width):
-                acc = acc_pool.tile([P, BANK], F32, name="acc", tag="acc")
-                first = piece * width
+            edges = [0]
+            for width, by_vector in PIECES.get(j, WHOLE_BANKS):
+                first = edges[-1]
+                edges.append(first + width)
+                acc = banks.tile([P, BANK], F32, name="acc", tag="bank")
                 nc.tensor.matmul_mx(
                     out=acc[:, 0:width],
                     lhsT=codes[:, j, :].bitcast(FP8X4),
@@ -164,18 +169,15 @@ def tile_mpnencoder_pa_kernel(tc, f_atoms, f_bonds, adj, w_words, w_scales, out)
                     stop=True,
                 )
                 columns = result[:, j, first : first + width]
-                if piece % 2 == 0:
+                if by_vector:
                     nc.vector.tensor_copy(out=columns, in_=acc[:, 0:width])
                 else:
                     nc.scalar.copy(out=columns, in_=acc[:, 0:width])
-                if j in PIECES:
-                    nc.sync.dma_start(out=out_rows[:, j, first : first + width], in_=columns)
-            if j in PIECES:
-                return
-            if j < JOIN_FROM:
-                nc.sync.dma_start(out=out_rows[:, j, :], in_=result[:, j, :])
-            elif (j - JOIN_FROM) % 2 == 1:
-                nc.sync.dma_start(out=out_rows[:, j - 1 : j + 1, :], in_=result[:, j - 1 : j + 1, :])
+            piece = 0
+            for count in STORES.get(j, (len(WHOLE_BANKS),)):
+                first, last = edges[piece], edges[piece + count]
+                nc.sync.dma_start(out=out_rows[:, j, first:last], in_=result[:, j, first:last])
+                piece += count
 
         halve_atoms()
         halve_bonds(1, BONDS_FIRST)
@@ -201,7 +203,7 @@ def tile_mpnencoder_pa_kernel(tc, f_atoms, f_bonds, adj, w_words, w_scales, out)
                 regroup(j + 3)
             if j + 2 < TILES:
                 quantise(j + 2)
-            if j + 4 < TILES:
+            if GATES_FIRST <= j + 4 < TILES:
                 gate(j + 4)
-            if j == 2:
+            if j == 3:
                 halve_bonds(BONDS_FIRST, TILES)

from contextlib import ExitStack

import concourse.mybir as mybir
from concourse.masks import make_identity

BF16 = mybir.dt.bfloat16
F32 = mybir.dt.float32
I32 = mybir.dt.int32
U32 = mybir.dt.uint32
U8 = mybir.dt.uint8
FP8X4 = mybir.dt.float8_e4m3fn_x4
FP4X4 = mybir.dt.float4_e2m1fn_x4
MULT = mybir.AluOpType.mult

P = 128
PAIRS = 2 * 32 * 32
TILES = PAIRS // P
ATOM = 352
TAIL = 96
BOND = 32
ATOMS = ATOM + TAIL
FEATURES = ATOMS + 2 * BOND
HALVES = 2
HIDDEN = 1024
BANK = 512
HALF = BANK // 2
PIECES = {
    0: ((HALF // 2, True), (HALF // 2, True), (HALF, False), (HALF, True), (HALF, False)),
    1: ((HALF, True), (HALF, False), (HALF, True), (HALF, False)),
}
WHOLE_BANKS = ((BANK, True), (BANK, False))
STORES = {0: (1, 1, 1, 2), 1: (2, 2)}
BONDS_FIRST = 8
GATES_FIRST = 6
WARM_FIRST = 9
WARM_SECOND = 4

FLOPS = 2 * PAIRS * FEATURES * HIDDEN


def tile_mpnencoder_pa_kernel(tc, f_atoms, f_bonds, adj, w_words, w_scales, out):
    nc = tc.nc

    with ExitStack() as ctx:
        keep = ctx.enter_context(tc.tile_pool(name="keep", bufs=1))
        banks = ctx.enter_context(tc.psum_pool(name="banks", bufs=8))
        ctx.enter_context(tc.manual_schedule())

        adj_sb = keep.tile([P, TILES], BF16, name="adj_sb")
        atoms = keep.tile([P, ATOM], BF16, name="atoms")
        bonds = keep.tile([P, TILES, BOND], BF16, name="bonds")
        halved_atoms = keep.tile([P, HALVES, ATOMS // HALVES], BF16, name="halved_atoms")
        halved_bonds = keep.tile([P, TILES, HALVES, BOND // HALVES], BF16, name="halved_bonds")
        weight = keep.tile([P, 2 * HIDDEN], U8, name="weight", align_bytes=64)
        weight_scales = keep.tile([P, HIDDEN], U8, name="weight_scales", align_bytes=64)

        zeros = keep.tile([P, 2], BF16, name="zeros")
        nc.gpsimd.memset(zeros[:].bitcast(I32), 0)
        nc.vector.memset(weight_scales[:].bitcast(I32), 0)
        idle_sums = banks.tile([P, BANK], F32, name="idle_sums", tag="bank")

        def keep_warm(count):
            for i in range(count):
                nc.tensor.matmul(
                    out=idle_sums[:, 0 : BANK // 2],
                    lhsT=zeros[:, 0:1].to_broadcast([P, P]),
                    rhs=zeros[:, 0:1].to_broadcast([P, BANK // 2]),
                    start=True,
                    stop=True,
                )

        keep_warm(WARM_FIRST)

        atom_rows = f_atoms.rearrange("b m f -> (b m) f")
        nc.sync.dma_start(
            out=atoms[:], in_=atom_rows.unsqueeze(1).to_broadcast([P // 2, 2, ATOM])
        )
        nc.sync.dma_start(out=adj_sb[:], in_=adj.rearrange("b m (h j) -> (b m h) j", j=TILES))
        bond_rows = f_bonds.rearrange("b m (h j) f -> (b m h) j f", j=TILES)
        nc.sync.dma_start(out=bonds[:, 0:BONDS_FIRST, :], in_=bond_rows[:, 0:BONDS_FIRST, :])
        nc.sync.dma_start(out=weight[:].bitcast(I32), in_=w_words[0].bitcast(I32))
        for q in range(4):
            nc.sync.dma_start(
                out=weight_scales[32 * q : 32 * q + 4, :].bitcast(I32),
                in_=w_scales[0, 4 * q : 4 * q + 4, :].bitcast(I32),
            )
        nc.sync.dma_start(out=bonds[:, BONDS_FIRST:TILES, :], in_=bond_rows[:, BONDS_FIRST:TILES, :])

        identity = keep.tile([P, P], F32, name="identity")
        make_identity(nc, identity[:])

        gated = keep.tile([P, TILES, FEATURES], BF16, name="gated")
        grouped = keep.tile([P, TILES, PAIRS // TILES * 4], BF16, name="grouped", align_bytes=64)
        codes = keep.tile([P, TILES, P], U32, name="codes", align_bytes=64)
        scales = keep.tile([P, TILES, P], U8, name="scales", align_bytes=64)
        result = keep.tile([P, TILES, HIDDEN], F32, name="result", align_bytes=256)
        out_rows = out.rearrange("b m (h j) c -> (b m h) j c", j=TILES)
        flipped = {}

        def halve_atoms():
            halved = halved_atoms[:].bitcast(F32)
            words = atoms[:].bitcast(F32).rearrange("p (w u) -> p u w", u=HALVES)
            first = ATOM // 4
            nc.scalar.copy(out=halved[:, :, 0:first], in_=words)
            nc.scalar.copy(out=halved[:, :, first:], in_=words[:, :, first - TAIL // 4 : first])

        def halve_bonds(begin, end):
            nc.scalar.copy(
                out=halved_bonds[:, begin:end].bitcast(F32),
                in_=bonds[:, begin:end].bitcast(F32).rearrange("p j (w u) -> p j u w", u=HALVES),
            )

        def gate(j):
            weight_of_pair = adj_sb[:, j : j + 1]

            def times(out, features):
                nc.vector.tensor_scalar(out=out, in0=features, scalar1=weight_of_pair, scalar2=None, op0=MULT)

            if j == 0:
                times(gated[:, j, 0:ATOM], atoms[:])
                times(gated[:, j, ATOM:ATOMS], atoms[:, ATOM - TAIL : ATOM])
                times(
                    gated[:, j, ATOMS:FEATURES].rearrange("p (d f) -> p d f", d=2),
                    bonds[:, j, :].unsqueeze(1).to_broadcast([P, 2, BOND]),
                )
            else:
                halves = gated[:, j, :].rearrange("p (u f) -> p u f", u=HALVES)
                times(halves[:, :, 0 : ATOMS // HALVES], halved_atoms[:])
                times(
                    halves[:, :, ATOMS // HALVES :].rearrange("p u (d f) -> p u d f", d=2),
                    halved_bonds[:, j].unsqueeze(2).to_broadcast([P, HALVES, 2, BOND // HALVES]),
                )

        def flip(*tiles):
            bank = banks.tile([P, BANK], F32, name="bank", tag="bank")
            for i, j in enumerate(tiles):
                flipped[j] = bank[:, i * HALVES * P : (i + 1) * HALVES * P]
                words = gated[:, j, :].bitcast(F32)
                for u in range(HALVES):
                    half = words[:, u : FEATURES // 2 : HALVES] if j == 0 else words[:, u * P : (u + 1) * P]
                    nc.tensor.transpose(flipped[j][:, u * P : (u + 1) * P], half, identity[:])

        def regroup(j):
            nc.scalar.copy(
                out=grouped[:, j, :].bitcast(F32).rearrange("k (p u) -> k p u", u=HALVES),
                in_=flipped[j].rearrange("k (u p) -> k p u", u=HALVES),
            )

        def quantise(j):
            nc.vector.quantize_mx(
                out=codes[:, j, :].bitcast(FP8X4),
                scales=scales[:, j, :],
                in_=grouped[:, j, :],
            )

        def project(j):
            edges = [0]
            for width, by_vector in PIECES.get(j, WHOLE_BANKS):
                first = edges[-1]
                edges.append(first + width)
                acc = banks.tile([P, BANK], F32, name="acc", tag="bank")
                nc.tensor.matmul_mx(
                    out=acc[:, 0:width],
                    lhsT=codes[:, j, :].bitcast(FP8X4),
                    lhsT_scale=scales[:, j, :],
                    rhs=weight[:, 2 * first : 2 * (first + width)].bitcast(FP4X4),
                    rhs_scale=weight_scales[:, first : first + width],
                    start=True,
                    stop=True,
                )
                columns = result[:, j, first : first + width]
                if by_vector:
                    nc.vector.tensor_copy(out=columns, in_=acc[:, 0:width])
                else:
                    nc.scalar.copy(out=columns, in_=acc[:, 0:width])
            piece = 0
            for count in STORES.get(j, (len(WHOLE_BANKS),)):
                first, last = edges[piece], edges[piece + count]
                nc.sync.dma_start(out=out_rows[:, j, first:last], in_=result[:, j, first:last])
                piece += count

        halve_atoms()
        halve_bonds(1, BONDS_FIRST)
        for j in range(GATES_FIRST):
            gate(j)
        flip(0)
        regroup(0)
        flip(1, 2)
        regroup(1)
        regroup(2)
        flip(3)
        regroup(3)
        keep_warm(WARM_SECOND)
        quantise(0)
        quantise(1)
        for j in range(TILES):
            project(j)
            if j == 0:
                quantise(2)
                continue
            if j + 3 < TILES:
                flip(j + 3)
                regroup(j + 3)
            if j + 2 < TILES:
                quantise(j + 2)
            if GATES_FIRST <= j + 4 < TILES:
                gate(j + 4)
            if j == 3:
                halve_bonds(BONDS_FIRST, TILES)
